import numpy as np
import ml_dtypes


def mxq(x, axis, fmt="e4m3"):
    dtype, down = {"e4m3": (ml_dtypes.float8_e4m3fn, 7), "e5m2": (ml_dtypes.float8_e5m2, 14)}[fmt]
    v = np.moveaxis(np.asarray(x, np.float32).astype(ml_dtypes.bfloat16).astype(np.float64), axis, -1)
    blocks = v.reshape(v.shape[:-1] + (-1, 32))
    amax = np.abs(blocks).max(-1, keepdims=True)
    byte = np.maximum(np.where(amax > 0, np.frexp(amax)[1] - 1 + 127, 0) - down, 1)
    scale = np.exp2(byte - 127.0)
    codes = (blocks / scale).astype(np.float32).astype(dtype).astype(np.float64)
    return np.moveaxis((codes * scale).reshape(v.shape), -1, axis)


WIDE = False


def mx_kscale(k):
    if not WIDE:
        return np.ones(k)
    levels = np.array([10, -10, 5, -5, 0])
    if k % 512:
        return np.exp2(np.random.permutation(np.resize(levels, k // 32))).repeat(32)
    a = np.empty((k // 512, 16))
    for p in range(k // 512):
        a[p, :8] = np.random.permutation(np.resize(levels, 8))
        for g in range(8):
            far = levels[np.abs(levels - a[p, g]) >= 10]
            a[p, g + 8] = far[np.random.randint(len(far))]
    return np.exp2(a.ravel()).repeat(32)


BF16 = ml_dtypes.bfloat16


def bf(x):
    return np.asarray(x, np.float32).astype(BF16)


def f64(x):
    return np.asarray(x).astype(np.float64)


B, K, H, D = 128, 128, 8192, 4
C = 0.2
HALF_LOG_2PI = 0.5 * np.log(2.0 * np.pi)


def log_softmax(v, axis):
    v = v - v.max(axis=axis, keepdims=True)
    return v - np.log(np.exp(v).sum(axis=axis, keepdims=True))


def logsumexp(v, axis):
    m = v.max(axis=axis, keepdims=True)
    return np.log(np.exp(v - m).sum(axis=axis)) + np.squeeze(m, axis)


def contract(xq, vq):
    return (xq.transpose(2, 0, 1) @ vq.transpose(2, 1, 0)).transpose(1, 2, 0)


def setup_inputs():
    s = mx_kscale(H)[None, :, None]
    r = 1.0 / np.sqrt(H)
    return {
        "x": bf(np.random.standard_normal((B, H, D)) * s),
        "input_var": bf(np.random.standard_normal((B, D)) * C),
        "V_alpha": bf(np.random.standard_normal((K, H, D)) * r / s),
        "V_mu": bf(np.random.standard_normal((K, H, D)) * C * r / s),
        "V_sigma": bf(np.random.standard_normal((K, H, D)) * 0.5 * r / s),
        "b_alpha": bf(np.random.standard_normal((K, D)) * 0.7),
        "b_mu": bf(np.random.standard_normal((K, D)) * 0.5 * C),
        "b_sigma": bf(np.log(C) + np.random.standard_normal((K, D)) * 0.3),
    }


def reference(x, input_var, V_alpha, V_mu, V_sigma, b_alpha, b_mu, b_sigma):
    xq = mxq(f64(x), 1, "e4m3")
    exp_alpha = contract(xq, mxq(f64(V_alpha), 1, "e4m3")) + f64(b_alpha)
    log_alpha = log_softmax(exp_alpha, 1)
    mu = contract(xq, mxq(f64(V_mu), 1, "e4m3")) + f64(b_mu)
    log_sigma = np.clip(contract(xq, mxq(f64(V_sigma), 1, "e4m3")) + f64(b_sigma), -20.0, 20.0)
    sigma = np.exp(log_sigma)
    y = f64(input_var)[:, None, :]
    log_p = -0.5 * np.square((y - mu) / sigma) + log_alpha - HALF_LOG_2PI - log_sigma
    return np.sum(logsumexp(log_p, 1), axis=1)

@@ -1,0 +1,255 @@
+import math
+from contextlib import ExitStack
+
+import concourse.mybir as mybir
+from concourse.masks import make_identity
+
+BF16 = mybir.dt.bfloat16
+F32 = mybir.dt.float32
+U32 = mybir.dt.uint32
+U8 = mybir.dt.uint8
+FP8X4 = mybir.dt.float8_e4m3fn_x4
+ALU = mybir.AluOpType
+ACT = mybir.ActivationFunctionType
+AXIS = mybir.AxisListType
+
+P = 128
+ROWS = 128
+H = 8192
+D = 4
+PACK = 4
+CHUNK = P * PACK
+CHUNKS = H // CHUNK
+PAIR = 2
+HALVES = D // PAIR
+STEPS = CHUNKS * HALVES
+SLOTS = 4
+X_SLOT = 0
+WEIGHTS = SLOTS - 1
+LOAD_CHUNKS = 1
+LOAD_H = LOAD_CHUNKS * CHUNK
+VECTOR_BANKS = 3
+SHARE_OF = 8
+HALF_LOG_2PI = 0.5 * math.log(2.0 * math.pi)
+
+FLOPS = 2 * WEIGHTS * D * ROWS * ROWS * H
+
+
+def tile_rnadeoutputlayer_k_kernel(
+    tc, x, input_var, V_alpha, V_mu, V_sigma, b_alpha, b_mu, b_sigma, out
+):
+    nc = tc.nc
+    operands = [x, V_alpha, V_mu, V_sigma]
+    biases = [b_alpha, b_mu, b_sigma]
+
+    with ExitStack() as ctx:
+        const = ctx.enter_context(tc.tile_pool(name="const", bufs=1))
+        raw_pool = ctx.enter_context(tc.tile_pool(name="raw", bufs=6))
+        stage = ctx.enter_context(tc.tile_pool(name="stage", bufs=3))
+        tail = ctx.enter_context(tc.tile_pool(name="tail", bufs=1))
+        acc_pool = ctx.enter_context(tc.psum_pool(name="acc", bufs=1))
+        bank_pool = ctx.enter_context(tc.psum_pool(name="banks", bufs=5))
+        ctx.enter_context(tc.manual_schedule())
+
+        ident = const.tile([P, P], F32)
+        make_identity(nc, ident[:])
+
+        warm = const.tile([P, 1], F32)
+        nc.vector.memset(warm[:], 0.0)
+        nc.scalar.activation(out=warm[:], in_=warm[:], func=ACT.Exp)
+
+        acc_alpha_mu = [
+            acc_pool.tile([P, PAIR, 2, ROWS], F32, name="acc_alpha_mu%d" % half) for half in range(HALVES)
+        ]
+        acc_sigma = acc_pool.tile([P, D, ROWS], F32)
+
+        bias_bf = const.tile([P, WEIGHTS, ROWS, D], BF16)
+        y_bf = const.tile([P, D], BF16)
+
+        raw = {}
+        grouped = {}
+        codes = {}
+        scales = {}
+
+        def load(group):
+            for slot in range(SLOTS):
+                raw[slot] = raw_pool.tile([P, LOAD_H * D], BF16, name="raw%d" % slot)
+                rows = operands[slot].rearrange("r h d -> r (h d)")
+                nc.sync.dma_start(
+                    out=raw[slot][:],
+                    in_=rows[:, group * LOAD_H * D : (group + 1) * LOAD_H * D],
+                )
+
+        def load_small():
+            for w in range(WEIGHTS):
+                nc.sync.dma_start(
+                    out=bias_bf[:, w, :, :].rearrange("p k d -> p (k d)"),
+                    in_=biases[w].rearrange("k d -> (k d)").partition_broadcast(P),
+                )
+            nc.sync.dma_start(out=y_bf[:], in_=input_var)
+
+        def transpose_and_regroup(step):
+            chunk, half = divmod(step, HALVES)
+            first_h = (chunk % LOAD_CHUNKS) * CHUNK
+            grouped[step] = stage.tile(
+                [P, PAIR, SLOTS, ROWS, PACK], BF16, name="grouped", align_bytes=64
+            )
+            for slot in range(SLOTS):
+                words = raw[slot][:].bitcast(F32).rearrange("p (h w) -> p w h", w=HALVES)
+                bank = bank_pool.tile([P, PACK, ROWS], F32, name="bank")
+                for t in range(PACK):
+                    nc.tensor.transpose(
+                        bank[:, t, :],
+                        words[:, half, first_h + t : first_h + CHUNK : PACK],
+                        ident[:],
+                    )
+                source = bank[:].bitcast(BF16).rearrange("p t (r e) -> p e r t", e=PAIR)
+                target = grouped[step][:, :, slot, :, :]
+                number = step * SLOTS + slot
+                if (number * VECTOR_BANKS) % SHARE_OF < VECTOR_BANKS:
+                    nc.vector.tensor_copy(out=target, in_=source)
+                else:
+                    nc.scalar.copy(out=target, in_=source)
+
+        def quantise(step):
+            codes[step] = stage.tile([P, PAIR, SLOTS * ROWS], U32, name="codes", align_bytes=64)
+            scales[step] = stage.tile([P, PAIR, SLOTS * ROWS], U8, name="scales", align_bytes=64)
+            nc.vector.quantize_mx(
+                out=codes[step][:].rearrange("p e c -> p (e c)").bitcast(FP8X4),
+                scales=scales[step][:].rearrange("p e c -> p (e c)"),
+                in_=grouped[step][:].rearrange("p e s r t -> p (e s r t)"),
+            )
+
+        def multiply(step):
+            chunk, half = divmod(step, HALVES)
+            x_cols = slice(X_SLOT * ROWS, (X_SLOT + 1) * ROWS)
+            alpha_mu_cols = slice(1 * ROWS, 3 * ROWS)
+            sigma_cols = slice(3 * ROWS, 4 * ROWS)
+            for e in range(PAIR):
+                first_e = e == 0
+                last_e = e == PAIR - 1
+                nc.tensor.matmul_mx(
+                    out=acc_sigma[:, half * PAIR + e, :],
+                    lhsT=codes[step][:, e, x_cols].bitcast(FP8X4),
+                    lhsT_scale=scales[step][:, e, x_cols],
+                    rhs=codes[step][:, e, sigma_cols].bitcast(FP8X4),
+                    rhs_scale=scales[step][:, e, sigma_cols],
+                    start=(step == 0 and first_e),
+                    stop=(step == STEPS - 1 and last_e),
+                )
+                nc.tensor.matmul_mx(
+                    out=acc_alpha_mu[half][:, e, :, :].rearrange("p w k -> p (w k)"),
+                    lhsT=codes[step][:, e, x_cols].bitcast(FP8X4),
+                    lhsT_scale=scales[step][:, e, x_cols],
+                    rhs=codes[step][:, e, alpha_mu_cols].bitcast(FP8X4),
+                    rhs_scale=scales[step][:, e, alpha_mu_cols],
+                    start=(chunk == 0 and first_e),
+                    stop=(chunk == CHUNKS - 1 and last_e),
+                )
+
+        for step in range(STEPS + 2):
+            if step < STEPS:
+                if step % (LOAD_CHUNKS * HALVES) == 0:
+                    load(step // (LOAD_CHUNKS * HALVES))
+                transpose_and_regroup(step)
+            if 1 <= step <= STEPS:
+                quantise(step - 1)
+            if step >= 2:
+                multiply(step - 2)
+
+        load_small()
+
+        A, Q = 0, 1
+        neg_max = tail.tile([P, 2, D], F32)
+        sums = tail.tile([P, 2, D], F32)
+        spent = tail.tile([P, ROWS], F32)
+        z = tail.tile([P, D, 2, ROWS], F32)
+        penalty = tail.tile([P, D, ROWS], F32)
+
+        y_scaled = tail.tile([P, D], F32)
+        nc.vector.tensor_scalar_mul(out=y_scaled[:], in0=y_bf[:], scalar1=-math.sqrt(0.5))
+
+        def fetch_alpha_mu(half):
+            of_half = slice(half * PAIR, (half + 1) * PAIR)
+            nc.vector.tensor_tensor(
+                out=z[:, of_half, :, :],
+                in0=acc_alpha_mu[half][:],
+                in1=bias_bf[:, 0:2, :, of_half].rearrange("p w k e -> p e w k"),
+                op=ALU.add,
+            )
+            for d in range(half * PAIR, (half + 1) * PAIR):
+                nc.scalar.activation(
+                    out=penalty[:, d, :],
+                    in_=z[:, d, 1, :],
+                    func=ACT.Square,
+                    scale=math.sqrt(0.5),
+                    bias=y_scaled[:, d : d + 1],
+                )
+
+        fetch_alpha_mu(0)
+
+        log_sigma = tail.tile([P, D, ROWS], F32)
+        nc.vector.tensor_tensor(
+            out=log_sigma[:],
+            in0=acc_sigma[:],
+            in1=bias_bf[:, 2, :, :].rearrange("p k d -> p d k"),
+            op=ALU.add,
+        )
+        nc.vector.tensor_scalar(
+            out=log_sigma[:], in0=log_sigma[:], scalar1=20.0, scalar2=-20.0, op0=ALU.min, op1=ALU.max
+        )
+        inv_variance = tail.tile([P, D, ROWS], F32)
+        nc.scalar.activation(out=inv_variance[:], in_=log_sigma[:], func=ACT.Exp, scale=-2.0)
+
+        fetch_alpha_mu(1)
+        a = z[:, :, 0, :]
+        q = tail.tile([P, D, ROWS], F32)
+
+        def sum_of_exponentials(which, logits):
+            for d in range(D):
+                nc.scalar.activation(
+                    out=spent[:],
+                    in_=logits[:, d, :],
+                    func=ACT.Exp,
+                    bias=neg_max[:, which, d : d + 1],
+                    accum_out=sums[:, which, d : d + 1],
+                )
+
+        nc.vector.tensor_reduce(out=neg_max[:, A, :], in_=a, axis=AXIS.X, op=ALU.max, negate=True)
+        sum_of_exponentials(A, a)
+        nc.vector.tensor_tensor(out=q[:], in0=a, in1=log_sigma[:], op=ALU.subtract)
+        nc.vector.tensor_tensor(out=penalty[:], in0=penalty[:], in1=inv_variance[:], op=ALU.mult)
+        nc.vector.tensor_tensor(out=q[:], in0=q[:], in1=penalty[:], op=ALU.subtract)
+        nc.vector.tensor_reduce(out=neg_max[:, Q, :], in_=q[:], axis=AXIS.X, op=ALU.max, negate=True)
+        sum_of_exponentials(Q, q[:])
+
+        neg_max_over_d = tail.tile([P, 2], F32)
+        nc.vector.tensor_reduce(out=neg_max_over_d[:], in_=neg_max[:], axis=AXIS.X, op=ALU.add)
+        offset = tail.tile([P, 1], F32)
+        nc.vector.tensor_scalar(
+            out=offset[:],
+            in0=neg_max_over_d[:, A : A + 1],
+            scalar1=neg_max_over_d[:, Q : Q + 1],
+            scalar2=-D * HALF_LOG_2PI,
+            op0=ALU.subtract,
+            op1=ALU.add,
+        )
+        logs = tail.tile([P, 2, D], F32)
+        nc.scalar.activation(out=logs[:], in_=sums[:], func=ACT.Ln)
+        logs_over_d = tail.tile([P, 2], F32)
+        nc.vector.tensor_reduce(out=logs_over_d[:], in_=logs[:], axis=AXIS.X, op=ALU.add)
+
+        repeated = tail.tile([P, P], F32)
+        nc.vector.tensor_scalar(
+            out=repeated[:],
+            in0=logs_over_d[:, Q : Q + 1].to_broadcast([P, P]),
+            scalar1=logs_over_d[:, A : A + 1],
+            scalar2=offset[:, 0:1],
+            op0=ALU.subtract,
+            op1=ALU.add,
+        )
+        row_bank = bank_pool.tile([P, PACK, ROWS], F32, name="bank")
+        nc.tensor.transpose(row_bank[:, 0, :], repeated[:], ident[:])
+        row = tail.tile([P, P], F32)
+        nc.vector.tensor_copy(out=row[:], in_=row_bank[:, 0, :])
+        nc.sync.dma_start(out=out.rearrange("(o b) -> o b", o=1), in_=row[0:1, :])

@@ -26,10 +26,10 @@ STEPS = CHUNKS * HALVES
 SLOTS = 4
 X_SLOT = 0
 WEIGHTS = SLOTS - 1
-LOAD_CHUNKS = 1
-LOAD_H = LOAD_CHUNKS * CHUNK
-VECTOR_BANKS = 3
-SHARE_OF = 8
+LAG = 2
+LAST_CHUNKS = 3
+VECTOR_BANKS = 1
+SHARE_OF = 3
 HALF_LOG_2PI = 0.5 * math.log(2.0 * math.pi)
 
 FLOPS = 2 * WEIGHTS * D * ROWS * ROWS * H
@@ -62,22 +62,28 @@ def tile_rnadeoutputlayer_k_kernel(
             acc_pool.tile([P, PAIR, 2, ROWS], F32, name="acc_alpha_mu%d" % half) for half in range(HALVES)
         ]
         acc_sigma = acc_pool.tile([P, D, ROWS], F32)
+        late_sigma = []
+        first_late = STEPS - LAST_CHUNKS
 
         bias_bf = const.tile([P, WEIGHTS, ROWS, D], BF16)
         y_bf = const.tile([P, D], BF16)
+
+        first_last = CHUNKS - LAST_CHUNKS
+        order = [(chunk, half) for chunk in range(first_last) for half in range(HALVES)]
+        order += [(chunk, half) for half in range(HALVES) for chunk in range(first_last, CHUNKS)]
 
         raw = {}
         grouped = {}
         codes = {}
         scales = {}
 
-        def load(group):
+        def load(chunk):
             for slot in range(SLOTS):
-                raw[slot] = raw_pool.tile([P, LOAD_H * D], BF16, name="raw%d" % slot)
+                raw[chunk, slot] = raw_pool.tile([P, CHUNK * D], BF16, name="raw%d" % slot)
                 rows = operands[slot].rearrange("r h d -> r (h d)")
                 nc.sync.dma_start(
-                    out=raw[slot][:],
-                    in_=rows[:, group * LOAD_H * D : (group + 1) * LOAD_H * D],
+                    out=raw[chunk, slot][:],
+                    in_=rows[:, chunk * CHUNK * D : (chunk + 1) * CHUNK * D],
                 )
 
         def load_small():
@@ -88,54 +94,59 @@ def tile_rnadeoutputlayer_k_kernel(
                 )
             nc.sync.dma_start(out=y_bf[:], in_=input_var)
 
-        def transpose_and_regroup(step):
-            chunk, half = divmod(step, HALVES)
-            first_h = (chunk % LOAD_CHUNKS) * CHUNK
-            grouped[step] = stage.tile(
-                [P, PAIR, SLOTS, ROWS, PACK], BF16, name="grouped", align_bytes=64
-            )
-            for slot in range(SLOTS):
-                words = raw[slot][:].bitcast(F32).rearrange("p (h w) -> p w h", w=HALVES)
-                bank = bank_pool.tile([P, PACK, ROWS], F32, name="bank")
-                for t in range(PACK):
-                    nc.tensor.transpose(
-                        bank[:, t, :],
-                        words[:, half, first_h + t : first_h + CHUNK : PACK],
-                        ident[:],
-                    )
-                source = bank[:].bitcast(BF16).rearrange("p t (r e) -> p e r t", e=PAIR)
-                target = grouped[step][:, :, slot, :, :]
-                number = step * SLOTS + slot
-                if (number * VECTOR_BANKS) % SHARE_OF < VECTOR_BANKS:
-                    nc.vector.tensor_copy(out=target, in_=source)
-                else:
-                    nc.scalar.copy(out=target, in_=source)
+        def transpose_and_regroup(step, slot):
+            chunk, half = order[step]
+            if slot == 0:
+                grouped[step] = stage.tile(
+                    [P, PAIR, SLOTS, ROWS, PACK], BF16, name="grouped", align_bytes=64
+                )
+            words = raw[chunk, slot][:].bitcast(F32).rearrange("p (h w) -> p w h", w=HALVES)
+            bank = bank_pool.tile([P, PACK, ROWS], F32, name="bank")
+            for t in range(PACK):
+                nc.tensor.transpose(bank[:, t, :], words[:, half, t:CHUNK:PACK], ident[:])
+            source = bank[:].bitcast(BF16).rearrange("p t (r e) -> p e r t", e=PAIR)
+            target = grouped[step][:, :, slot, :, :]
+            if chunk == 0:
+                on_vector = half == 0
+            elif step >= first_late:
+                on_vector = slot == 0
+            else:
+                on_vector = ((step * SLOTS + slot) * VECTOR_BANKS) % SHARE_OF < VECTOR_BANKS
+            if on_vector:
+                nc.vector.tensor_copy(out=target, in_=source)
+            else:
+                nc.scalar.copy(out=target, in_=source)
 
         def quantise(step):
             codes[step] = stage.tile([P, PAIR, SLOTS * ROWS], U32, name="codes", align_bytes=64)
             scales[step] = stage.tile([P, PAIR, SLOTS * ROWS], U8, name="scales", align_bytes=64)
-            nc.vector.quantize_mx(
-                out=codes[step][:].rearrange("p e c -> p (e c)").bitcast(FP8X4),
-                scales=scales[step][:].rearrange("p e c -> p (e c)"),
-                in_=grouped[step][:].rearrange("p e s r t -> p (e s r t)"),
-            )
+            width = 1 if step == STEPS - 1 else PAIR
+            for e in range(0, PAIR, width):
+                part = slice(e, e + width)
+                nc.vector.quantize_mx(
+                    out=codes[step][:, part, :].rearrange("p e c -> p (e c)").bitcast(FP8X4),
+                    scales=scales[step][:, part, :].rearrange("p e c -> p (e c)"),
+                    in_=grouped[step][:, part, :, :, :].rearrange("p e s r t -> p (e s r t)"),
+                )
 
         def multiply(step):
-            chunk, half = divmod(step, HALVES)
+            chunk, half = order[step]
             x_cols = slice(X_SLOT * ROWS, (X_SLOT + 1) * ROWS)
             alpha_mu_cols = slice(1 * ROWS, 3 * ROWS)
             sigma_cols = slice(3 * ROWS, 4 * ROWS)
+            if step == first_late:
+                late_sigma.append(bank_pool.tile([P, PACK, ROWS], F32, name="bank"))
             for e in range(PAIR):
                 first_e = e == 0
                 last_e = e == PAIR - 1
                 nc.tensor.matmul_mx(
-                    out=acc_sigma[:, half * PAIR + e, :],
+                    out=late_sigma[0][:, e, :] if step >= first_late else acc_sigma[:, half * PAIR + e, :],
                     lhsT=codes[step][:, e, x_cols].bitcast(FP8X4),
                     lhsT_scale=scales[step][:, e, x_cols],
                     rhs=codes[step][:, e, sigma_cols].bitcast(FP8X4),
                     rhs_scale=scales[step][:, e, sigma_cols],
-                    start=(step == 0 and first_e),
-                    stop=(step == STEPS - 1 and last_e),
+                    start=(step in (0, first_late) and first_e),
+                    stop=(step in (first_late - 1, STEPS - 1) and last_e),
                 )
                 nc.tensor.matmul_mx(
                     out=acc_alpha_mu[half][:, e, :, :].rearrange("p w k -> p (w k)"),
@@ -147,35 +158,60 @@ def tile_rnadeoutputlayer_k_kernel(
                     stop=(chunk == CHUNKS - 1 and last_e),
                 )
 
-        for step in range(STEPS + 2):
-            if step < STEPS:
-                if step % (LOAD_CHUNKS * HALVES) == 0:
-                    load(step // (LOAD_CHUNKS * HALVES))
-                transpose_and_regroup(step)
-            if 1 <= step <= STEPS:
-                quantise(step - 1)
-            if step >= 2:
-                multiply(step - 2)
-
-        load_small()
-
         A, Q = 0, 1
         neg_max = tail.tile([P, 2, D], F32)
         sums = tail.tile([P, 2, D], F32)
         spent = tail.tile([P, ROWS], F32)
         z = tail.tile([P, D, 2, ROWS], F32)
         penalty = tail.tile([P, D, ROWS], F32)
-
+        log_sigma = tail.tile([P, D, ROWS], F32)
+        inv_variance = tail.tile([P, D, ROWS], F32)
+        q = tail.tile([P, D, ROWS], F32)
         y_scaled = tail.tile([P, D], F32)
-        nc.vector.tensor_scalar_mul(out=y_scaled[:], in0=y_bf[:], scalar1=-math.sqrt(0.5))
 
-        def fetch_alpha_mu(half):
+        def sum_of_exponentials(which, logits, half):
+            for e in range(PAIR):
+                d = half * PAIR + e
+                nc.scalar.activation(
+                    out=spent[:],
+                    in_=logits[:, e, :],
+                    func=ACT.Exp,
+                    bias=neg_max[:, which, d : d + 1],
+                    accum_out=sums[:, which, d : d + 1],
+                )
+
+        def fetch_sums(half):
             of_half = slice(half * PAIR, (half + 1) * PAIR)
+            if half == 0:
+                nc.vector.tensor_tensor(
+                    out=log_sigma[:],
+                    in0=acc_sigma[:],
+                    in1=bias_bf[:, 2, :, :].rearrange("p k d -> p d k"),
+                    op=ALU.add,
+                )
+            else:
+                nc.vector.tensor_tensor(
+                    out=log_sigma[:, of_half, :],
+                    in0=late_sigma[0][:, 0:PAIR, :],
+                    in1=log_sigma[:, of_half, :],
+                    op=ALU.add,
+                )
             nc.vector.tensor_tensor(
                 out=z[:, of_half, :, :],
                 in0=acc_alpha_mu[half][:],
                 in1=bias_bf[:, 0:2, :, of_half].rearrange("p w k e -> p e w k"),
                 op=ALU.add,
+            )
+            nc.vector.tensor_scalar(
+                out=log_sigma[:, of_half, :],
+                in0=log_sigma[:, of_half, :],
+                scalar1=20.0,
+                scalar2=-20.0,
+                op0=ALU.min,
+                op1=ALU.max,
+            )
+            nc.vector.tensor_reduce(
+                out=neg_max[:, A, of_half], in_=z[:, of_half, 0, :], axis=AXIS.X, op=ALU.max, negate=True
             )
             for d in range(half * PAIR, (half + 1) * PAIR):
                 nc.scalar.activation(
@@ -185,71 +221,84 @@ def tile_rnadeoutputlayer_k_kernel(
                     scale=math.sqrt(0.5),
                     bias=y_scaled[:, d : d + 1],
                 )
+            nc.scalar.activation(
+                out=inv_variance[:, of_half, :], in_=log_sigma[:, of_half, :], func=ACT.Exp, scale=-2.0
+            )
+            sum_of_exponentials(A, z[:, of_half, 0, :], half)
 
-        fetch_alpha_mu(0)
+        def finish_half(half):
+            of_half = slice(half * PAIR, (half + 1) * PAIR)
+            nc.vector.tensor_tensor(
+                out=q[:, of_half, :], in0=z[:, of_half, 0, :], in1=log_sigma[:, of_half, :], op=ALU.subtract
+            )
+            nc.vector.tensor_tensor(
+                out=penalty[:, of_half, :],
+                in0=penalty[:, of_half, :],
+                in1=inv_variance[:, of_half, :],
+                op=ALU.mult,
+            )
+            nc.vector.tensor_tensor(
+                out=q[:, of_half, :], in0=q[:, of_half, :], in1=penalty[:, of_half, :], op=ALU.subtract
+            )
+            nc.vector.tensor_reduce(
+                out=neg_max[:, Q, of_half], in_=q[:, of_half, :], axis=AXIS.X, op=ALU.max, negate=True
+            )
+            sum_of_exponentials(Q, q[:, of_half, :], half)
 
-        log_sigma = tail.tile([P, D, ROWS], F32)
-        nc.vector.tensor_tensor(
-            out=log_sigma[:],
-            in0=acc_sigma[:],
-            in1=bias_bf[:, 2, :, :].rearrange("p k d -> p d k"),
-            op=ALU.add,
-        )
-        nc.vector.tensor_scalar(
-            out=log_sigma[:], in0=log_sigma[:], scalar1=20.0, scalar2=-20.0, op0=ALU.min, op1=ALU.max
-        )
-        inv_variance = tail.tile([P, D, ROWS], F32)
-        nc.scalar.activation(out=inv_variance[:], in_=log_sigma[:], func=ACT.Exp, scale=-2.0)
-
-        fetch_alpha_mu(1)
-        a = z[:, :, 0, :]
-        q = tail.tile([P, D, ROWS], F32)
-
-        def sum_of_exponentials(which, logits):
-            for d in range(D):
-                nc.scalar.activation(
-                    out=spent[:],
-                    in_=logits[:, d, :],
-                    func=ACT.Exp,
-                    bias=neg_max[:, which, d : d + 1],
-                    accum_out=sums[:, which, d : d + 1],
-                )
-
-        nc.vector.tensor_reduce(out=neg_max[:, A, :], in_=a, axis=AXIS.X, op=ALU.max, negate=True)
-        sum_of_exponentials(A, a)
-        nc.vector.tensor_tensor(out=q[:], in0=a, in1=log_sigma[:], op=ALU.subtract)
-        nc.vector.tensor_tensor(out=penalty[:], in0=penalty[:], in1=inv_variance[:], op=ALU.mult)
-        nc.vector.tensor_tensor(out=q[:], in0=q[:], in1=penalty[:], op=ALU.subtract)
-        nc.vector.tensor_reduce(out=neg_max[:, Q, :], in_=q[:], axis=AXIS.X, op=ALU.max, negate=True)
-        sum_of_exponentials(Q, q[:])
+        load(0)
+        for slot in range(SLOTS):
+            for step in range(HALVES):
+                transpose_and_regroup(step, slot)
+        for step in range(1, STEPS + LAG):
+            if HALVES <= step < STEPS:
+                chunk, half = order[step]
+                if half == 0:
+                    load(chunk)
+                if step == first_late:
+                    load_small()
+                for slot in range(SLOTS):
+                    transpose_and_regroup(step, slot)
+            if step <= STEPS:
+                quantise(step - 1)
+            if step >= LAG:
+                multiply(step - LAG)
+            if step == first_late - 1 + LAG:
+                nc.vector.tensor_scalar_mul(out=y_scaled[:], in0=y_bf[:], scalar1=-math.sqrt(0.5))
+                fetch_sums(0)
+            if step == first_late + LAG:
+                finish_half(0)
+        fetch_sums(1)
+        finish_half(1)
 
         neg_max_over_d = tail.tile([P, 2], F32)
         nc.vector.tensor_reduce(out=neg_max_over_d[:], in_=neg_max[:], axis=AXIS.X, op=ALU.add)
-        offset = tail.tile([P, 1], F32)
+        offset = tail.tile([P, P], F32)
         nc.vector.tensor_scalar(
             out=offset[:],
-            in0=neg_max_over_d[:, A : A + 1],
+            in0=neg_max_over_d[:, A : A + 1].to_broadcast([P, P]),
             scalar1=neg_max_over_d[:, Q : Q + 1],
             scalar2=-D * HALF_LOG_2PI,
             op0=ALU.subtract,
             op1=ALU.add,
         )
-        logs = tail.tile([P, 2, D], F32)
-        nc.scalar.activation(out=logs[:], in_=sums[:], func=ACT.Ln)
-        logs_over_d = tail.tile([P, 2], F32)
-        nc.vector.tensor_reduce(out=logs_over_d[:], in_=logs[:], axis=AXIS.X, op=ALU.add)
+        offset_bank = bank_pool.tile([P, PACK, ROWS], F32, name="bank")
+        nc.tensor.transpose(offset_bank[:, 0, :], offset[:], ident[:])
+        offset_row = tail.tile([P, P], F32)
+        nc.vector.tensor_copy(out=offset_row[:], in_=offset_bank[:, 0, :])
 
-        repeated = tail.tile([P, P], F32)
-        nc.vector.tensor_scalar(
-            out=repeated[:],
-            in0=logs_over_d[:, Q : Q + 1].to_broadcast([P, P]),
-            scalar1=logs_over_d[:, A : A + 1],
-            scalar2=offset[:, 0:1],
-            op0=ALU.subtract,
-            op1=ALU.add,
+        pairs = tail.tile([P, 2, PAIR], F32)
+        nc.vector.tensor_tensor(out=pairs[:], in0=sums[:, :, 0:PAIR], in1=sums[:, :, PAIR:D], op=ALU.mult)
+        product = tail.tile([P, 2, 1], F32)
+        nc.vector.tensor_tensor(out=product[:], in0=pairs[:, :, 0:1], in1=pairs[:, :, 1:2], op=ALU.mult)
+        inverse = tail.tile([P, 1], F32)
+        nc.vector.reciprocal(out=inverse[:], in_=product[:, A, :])
+
+        logs = tail.tile([P, P], F32)
+        nc.scalar.activation(
+            out=logs[:], in_=product[:, Q, :].to_broadcast([P, P]), func=ACT.Ln, scale=inverse[:, 0:1]
         )
         row_bank = bank_pool.tile([P, PACK, ROWS], F32, name="bank")
-        nc.tensor.transpose(row_bank[:, 0, :], repeated[:], ident[:])
+        nc.tensor.transpose(row_bank[:, 0, :], logs[:], ident[:])
         row = tail.tile([P, P], F32)
-        nc.vector.tensor_copy(out=row[:], in_=row_bank[:, 0, :])
+        nc.vector.tensor_tensor(out=row[:], in0=row_bank[:, 0, :], in1=offset_row[:], op=ALU.add)
         nc.sync.dma_start(out=out.rearrange("(o b) -> o b", o=1), in_=row[0:1, :])

import math
from contextlib import ExitStack

import concourse.mybir as mybir
from concourse.masks import make_identity

BF16 = mybir.dt.bfloat16
F32 = mybir.dt.float32
U32 = mybir.dt.uint32
U8 = mybir.dt.uint8
FP8X4 = mybir.dt.float8_e4m3fn_x4
ALU = mybir.AluOpType
ACT = mybir.ActivationFunctionType
AXIS = mybir.AxisListType

P = 128
ROWS = 128
H = 8192
D = 4
PACK = 4
CHUNK = P * PACK
CHUNKS = H // CHUNK
PAIR = 2
HALVES = D // PAIR
STEPS = CHUNKS * HALVES
SLOTS = 4
X_SLOT = 0
WEIGHTS = SLOTS - 1
LAG = 2
LAST_CHUNKS = 3
VECTOR_BANKS = 1
SHARE_OF = 3
HALF_LOG_2PI = 0.5 * math.log(2.0 * math.pi)

FLOPS = 2 * WEIGHTS * D * ROWS * ROWS * H


def tile_rnadeoutputlayer_k_kernel(
    tc, x, input_var, V_alpha, V_mu, V_sigma, b_alpha, b_mu, b_sigma, out
):
    nc = tc.nc
    operands = [x, V_alpha, V_mu, V_sigma]
    biases = [b_alpha, b_mu, b_sigma]

    with ExitStack() as ctx:
        const = ctx.enter_context(tc.tile_pool(name="const", bufs=1))
        raw_pool = ctx.enter_context(tc.tile_pool(name="raw", bufs=6))
        stage = ctx.enter_context(tc.tile_pool(name="stage", bufs=3))
        tail = ctx.enter_context(tc.tile_pool(name="tail", bufs=1))
        acc_pool = ctx.enter_context(tc.psum_pool(name="acc", bufs=1))
        bank_pool = ctx.enter_context(tc.psum_pool(name="banks", bufs=5))
        ctx.enter_context(tc.manual_schedule())

        ident = const.tile([P, P], F32)
        make_identity(nc, ident[:])

        warm = const.tile([P, 1], F32)
        nc.vector.memset(warm[:], 0.0)
        nc.scalar.activation(out=warm[:], in_=warm[:], func=ACT.Exp)

        acc_alpha_mu = [
            acc_pool.tile([P, PAIR, 2, ROWS], F32, name="acc_alpha_mu%d" % half) for half in range(HALVES)
        ]
        acc_sigma = acc_pool.tile([P, D, ROWS], F32)
        late_sigma = []
        first_late = STEPS - LAST_CHUNKS

        bias_bf = const.tile([P, WEIGHTS, ROWS, D], BF16)
        y_bf = const.tile([P, D], BF16)

        first_last = CHUNKS - LAST_CHUNKS
        order = [(chunk, half) for chunk in range(first_last) for half in range(HALVES)]
        order += [(chunk, half) for half in range(HALVES) for chunk in range(first_last, CHUNKS)]

        raw = {}
        grouped = {}
        codes = {}
        scales = {}

        def load(chunk):
            for slot in range(SLOTS):
                raw[chunk, slot] = raw_pool.tile([P, CHUNK * D], BF16, name="raw%d" % slot)
                rows = operands[slot].rearrange("r h d -> r (h d)")
                nc.sync.dma_start(
                    out=raw[chunk, slot][:],
                    in_=rows[:, chunk * CHUNK * D : (chunk + 1) * CHUNK * D],
                )

        def load_small():
            for w in range(WEIGHTS):
                nc.sync.dma_start(
                    out=bias_bf[:, w, :, :].rearrange("p k d -> p (k d)"),
                    in_=biases[w].rearrange("k d -> (k d)").partition_broadcast(P),
                )
            nc.sync.dma_start(out=y_bf[:], in_=input_var)

        def transpose_and_regroup(step, slot):
            chunk, half = order[step]
            if slot == 0:
                grouped[step] = stage.tile(
                    [P, PAIR, SLOTS, ROWS, PACK], BF16, name="grouped", align_bytes=64
                )
            words = raw[chunk, slot][:].bitcast(F32).rearrange("p (h w) -> p w h", w=HALVES)
            bank = bank_pool.tile([P, PACK, ROWS], F32, name="bank")
            for t in range(PACK):
                nc.tensor.transpose(bank[:, t, :], words[:, half, t:CHUNK:PACK], ident[:])
            source = bank[:].bitcast(BF16).rearrange("p t (r e) -> p e r t", e=PAIR)
            target = grouped[step][:, :, slot, :, :]
            if chunk == 0:
                on_vector = half == 0
            elif step >= first_late:
                on_vector = slot == 0
            else:
                on_vector = ((step * SLOTS + slot) * VECTOR_BANKS) % SHARE_OF < VECTOR_BANKS
            if on_vector:
                nc.vector.tensor_copy(out=target, in_=source)
            else:
                nc.scalar.copy(out=target, in_=source)

        def quantise(step):
            codes[step] = stage.tile([P, PAIR, SLOTS * ROWS], U32, name="codes", align_bytes=64)
            scales[step] = stage.tile([P, PAIR, SLOTS * ROWS], U8, name="scales", align_bytes=64)
            width = 1 if step == STEPS - 1 else PAIR
            for e in range(0, PAIR, width):
                part = slice(e, e + width)
                nc.vector.quantize_mx(
                    out=codes[step][:, part, :].rearrange("p e c -> p (e c)").bitcast(FP8X4),
                    scales=scales[step][:, part, :].rearrange("p e c -> p (e c)"),
                    in_=grouped[step][:, part, :, :, :].rearrange("p e s r t -> p (e s r t)"),
                )

        def multiply(step):
            chunk, half = order[step]
            x_cols = slice(X_SLOT * ROWS, (X_SLOT + 1) * ROWS)
            alpha_mu_cols = slice(1 * ROWS, 3 * ROWS)
            sigma_cols = slice(3 * ROWS, 4 * ROWS)
            if step == first_late:
                late_sigma.append(bank_pool.tile([P, PACK, ROWS], F32, name="bank"))
            for e in range(PAIR):
                first_e = e == 0
                last_e = e == PAIR - 1
                nc.tensor.matmul_mx(
                    out=late_sigma[0][:, e, :] if step >= first_late else acc_sigma[:, half * PAIR + e, :],
                    lhsT=codes[step][:, e, x_cols].bitcast(FP8X4),
                    lhsT_scale=scales[step][:, e, x_cols],
                    rhs=codes[step][:, e, sigma_cols].bitcast(FP8X4),
                    rhs_scale=scales[step][:, e, sigma_cols],
                    start=(step in (0, first_late) and first_e),
                    stop=(step in (first_late - 1, STEPS - 1) and last_e),
                )
                nc.tensor.matmul_mx(
                    out=acc_alpha_mu[half][:, e, :, :].rearrange("p w k -> p (w k)"),
                    lhsT=codes[step][:, e, x_cols].bitcast(FP8X4),
                    lhsT_scale=scales[step][:, e, x_cols],
                    rhs=codes[step][:, e, alpha_mu_cols].bitcast(FP8X4),
                    rhs_scale=scales[step][:, e, alpha_mu_cols],
                    start=(chunk == 0 and first_e),
                    stop=(chunk == CHUNKS - 1 and last_e),
                )

        A, Q = 0, 1
        neg_max = tail.tile([P, 2, D], F32)
        sums = tail.tile([P, 2, D], F32)
        spent = tail.tile([P, ROWS], F32)
        z = tail.tile([P, D, 2, ROWS], F32)
        penalty = tail.tile([P, D, ROWS], F32)
        log_sigma = tail.tile([P, D, ROWS], F32)
        inv_variance = tail.tile([P, D, ROWS], F32)
        q = tail.tile([P, D, ROWS], F32)
        y_scaled = tail.tile([P, D], F32)

        def sum_of_exponentials(which, logits, half):
            for e in range(PAIR):
                d = half * PAIR + e
                nc.scalar.activation(
                    out=spent[:],
                    in_=logits[:, e, :],
                    func=ACT.Exp,
                    bias=neg_max[:, which, d : d + 1],
                    accum_out=sums[:, which, d : d + 1],
                )

        def fetch_sums(half):
            of_half = slice(half * PAIR, (half + 1) * PAIR)
            if half == 0:
                nc.vector.tensor_tensor(
                    out=log_sigma[:],
                    in0=acc_sigma[:],
                    in1=bias_bf[:, 2, :, :].rearrange("p k d -> p d k"),
                    op=ALU.add,
                )
            else:
                nc.vector.tensor_tensor(
                    out=log_sigma[:, of_half, :],
                    in0=late_sigma[0][:, 0:PAIR, :],
                    in1=log_sigma[:, of_half, :],
                    op=ALU.add,
                )
            nc.vector.tensor_tensor(
                out=z[:, of_half, :, :],
                in0=acc_alpha_mu[half][:],
                in1=bias_bf[:, 0:2, :, of_half].rearrange("p w k e -> p e w k"),
                op=ALU.add,
            )
            nc.vector.tensor_scalar(
                out=log_sigma[:, of_half, :],
                in0=log_sigma[:, of_half, :],
                scalar1=20.0,
                scalar2=-20.0,
                op0=ALU.min,
                op1=ALU.max,
            )
            nc.vector.tensor_reduce(
                out=neg_max[:, A, of_half], in_=z[:, of_half, 0, :], axis=AXIS.X, op=ALU.max, negate=True
            )
            for d in range(half * PAIR, (half + 1) * PAIR):
                nc.scalar.activation(
                    out=penalty[:, d, :],
                    in_=z[:, d, 1, :],
                    func=ACT.Square,
                    scale=math.sqrt(0.5),
                    bias=y_scaled[:, d : d + 1],
                )
            nc.scalar.activation(
                out=inv_variance[:, of_half, :], in_=log_sigma[:, of_half, :], func=ACT.Exp, scale=-2.0
            )
            sum_of_exponentials(A, z[:, of_half, 0, :], half)

        def finish_half(half):
            of_half = slice(half * PAIR, (half + 1) * PAIR)
            nc.vector.tensor_tensor(
                out=q[:, of_half, :], in0=z[:, of_half, 0, :], in1=log_sigma[:, of_half, :], op=ALU.subtract
            )
            nc.vector.tensor_tensor(
                out=penalty[:, of_half, :],
                in0=penalty[:, of_half, :],
                in1=inv_variance[:, of_half, :],
                op=ALU.mult,
            )
            nc.vector.tensor_tensor(
                out=q[:, of_half, :], in0=q[:, of_half, :], in1=penalty[:, of_half, :], op=ALU.subtract
            )
            nc.vector.tensor_reduce(
                out=neg_max[:, Q, of_half], in_=q[:, of_half, :], axis=AXIS.X, op=ALU.max, negate=True
            )
            sum_of_exponentials(Q, q[:, of_half, :], half)

        load(0)
        for slot in range(SLOTS):
            for step in range(HALVES):
                transpose_and_regroup(step, slot)
        for step in range(1, STEPS + LAG):
            if HALVES <= step < STEPS:
                chunk, half = order[step]
                if half == 0:
                    load(chunk)
                if step == first_late:
                    load_small()
                for slot in range(SLOTS):
                    transpose_and_regroup(step, slot)
            if step <= STEPS:
                quantise(step - 1)
            if step >= LAG:
                multiply(step - LAG)
            if step == first_late - 1 + LAG:
                nc.vector.tensor_scalar_mul(out=y_scaled[:], in0=y_bf[:], scalar1=-math.sqrt(0.5))
                fetch_sums(0)
            if step == first_late + LAG:
                finish_half(0)
        fetch_sums(1)
        finish_half(1)

        neg_max_over_d = tail.tile([P, 2], F32)
        nc.vector.tensor_reduce(out=neg_max_over_d[:], in_=neg_max[:], axis=AXIS.X, op=ALU.add)
        offset = tail.tile([P, P], F32)
        nc.vector.tensor_scalar(
            out=offset[:],
            in0=neg_max_over_d[:, A : A + 1].to_broadcast([P, P]),
            scalar1=neg_max_over_d[:, Q : Q + 1],
            scalar2=-D * HALF_LOG_2PI,
            op0=ALU.subtract,
            op1=ALU.add,
        )
        offset_bank = bank_pool.tile([P, PACK, ROWS], F32, name="bank")
        nc.tensor.transpose(offset_bank[:, 0, :], offset[:], ident[:])
        offset_row = tail.tile([P, P], F32)
        nc.vector.tensor_copy(out=offset_row[:], in_=offset_bank[:, 0, :])

        pairs = tail.tile([P, 2, PAIR], F32)
        nc.vector.tensor_tensor(out=pairs[:], in0=sums[:, :, 0:PAIR], in1=sums[:, :, PAIR:D], op=ALU.mult)
        product = tail.tile([P, 2, 1], F32)
        nc.vector.tensor_tensor(out=product[:], in0=pairs[:, :, 0:1], in1=pairs[:, :, 1:2], op=ALU.mult)
        inverse = tail.tile([P, 1], F32)
        nc.vector.reciprocal(out=inverse[:], in_=product[:, A, :])

        logs = tail.tile([P, P], F32)
        nc.scalar.activation(
            out=logs[:], in_=product[:, Q, :].to_broadcast([P, P]), func=ACT.Ln, scale=inverse[:, 0:1]
        )
        row_bank = bank_pool.tile([P, PACK, ROWS], F32, name="bank")
        nc.tensor.transpose(row_bank[:, 0, :], logs[:], ident[:])
        row = tail.tile([P, P], F32)
        nc.vector.tensor_tensor(out=row[:], in0=row_bank[:, 0, :], in1=offset_row[:], op=ALU.add)
        nc.sync.dma_start(out=out.rearrange("(o b) -> o b", o=1), in_=row[0:1, :])
